import numpy as np
import ml_dtypes


def mxq(x, axis, fmt="e4m3"):
    dtype, down = {"e4m3": (ml_dtypes.float8_e4m3fn, 7), "e5m2": (ml_dtypes.float8_e5m2, 14)}[fmt]
    v = np.moveaxis(np.asarray(x, np.float32).astype(ml_dtypes.bfloat16).astype(np.float64), axis, -1)
    blocks = v.reshape(v.shape[:-1] + (-1, 32))
    amax = np.abs(blocks).max(-1, keepdims=True)
    byte = np.maximum(np.where(amax > 0, np.frexp(amax)[1] - 1 + 127, 0) - down, 1)
    scale = np.exp2(byte - 127.0)
    codes = (blocks / scale).astype(np.float32).astype(dtype).astype(np.float64)
    return np.moveaxis((codes * scale).reshape(v.shape), -1, axis)


WIDE = False


def mx_kscale(k):
    if not WIDE:
        return np.ones(k)
    levels = np.array([10, -10, 5, -5, 0])
    a = np.random.permutation(np.resize(levels, k // 512 * 4)).reshape(k // 512, 4)
    idx = np.arange(k)
    return np.exp2(a[idx // 512, idx % 128 // 32])


BF16 = ml_dtypes.bfloat16


def bf(x):
    return np.asarray(x, np.float32).astype(BF16)


def f64(x):
    return np.asarray(x).astype(np.float64)


N, F, M, E, H, G, C = 2048, 1024, 512, 512, 256, 128, 10


def draw_adj():
    p = np.random.standard_normal(N)
    return np.exp(1.5 * np.random.standard_normal((N, N)) + 0.5 * p[:, None] + 0.5 * p[None, :]) * 0.3 / N


def setup_inputs():
    s = mx_kscale(N)
    c = s / np.exp2(np.round(np.log2(s.mean())))
    return {"h_gcn1": bf(np.maximum(np.random.standard_normal((N, H)), 0.0) / c[:, None]),
            "adj": bf(draw_adj() * c),
            "gcn2_w": bf(np.random.standard_normal((H, G)) * 1.5 / np.sqrt(H)),
            "gcn2_b": bf(np.random.standard_normal(G) * 0.1)}


def reference(h_gcn1, adj, gcn2_w, gcn2_b):
    a = f64(adj)
    deg = a.sum(axis=1)
    dis = deg ** -0.5
    xw = f64(h_gcn1) @ f64(gcn2_w)
    y = dis[:, None] * xw
    agg = mxq(a, 1, "e4m3") @ mxq(y, 0, "e4m3")
    return np.maximum(dis[:, None] * agg + f64(gcn2_b), 0.0)

@@ -1,0 +1,256 @@
+from contextlib import ExitStack
+
+import concourse.mybir as mybir
+from concourse.masks import make_identity
+
+F32 = mybir.dt.float32
+BF16 = mybir.dt.bfloat16
+U32 = mybir.dt.uint32
+U8 = mybir.dt.uint8
+FP8X4 = mybir.dt.float8_e4m3fn_x4
+ALU = mybir.AluOpType
+ACT = mybir.ActivationFunctionType
+
+P = 128
+N_NODES = 2048
+H_IN = 256
+G_OUT = 128
+TILES = 16
+PASSES = 4
+
+FLOPS = 2 * N_NODES * N_NODES * G_OUT + 2 * N_NODES * H_IN * G_OUT
+
+D_MODE = "VSVVSVVSVVSVVVVV"
+E_ENG = ("SS", "SS", "SS", "SS", "SS", "SS", "SS", "SS", "SS", "SS", "SS", "SS", "SS", "SS", "SS", "SS")
+H_AFTER = 3
+ORDER = (
+    ("T", 0, 0), ("D", 0, 0), ("T", 0, 1), ("E", 0, 0), ("T", 1, 0), ("D", 1, 0), ("T", 1, 1), ("T", 2, 0),
+    ("D", 2, 0), ("E", 0, 1), ("D", 3, 0), ("E", 1, 0), ("T", 2, 1), ("E", 1, 1), ("Q", 0, 0), ("T", 3, 0),
+    ("SQ", 0, 0), ("T", 3, 1), ("Q", 1, 0), ("E", 2, 0), ("RC", 0, 0), ("E", 2, 1), ("HT", 0, 0), ("E", 3, 0),
+    ("HT", 1, 0), ("Q", 2, 0), ("D", 4, 0), ("HT", 2, 0), ("D", 5, 0), ("E", 3, 1), ("D", 6, 0), ("HE", 0, 0),
+    ("HT", 3, 0), ("D", 7, 0), ("Q", 3, 0), ("XW", 0, 0), ("T", 4, 0), ("Y", 0, 0), ("QY", 0, 0), ("D", 8, 0),
+    ("SQ", 1, 0), ("HE", 1, 0), ("RC", 1, 0), ("HE", 2, 0), ("D", 9, 0), ("XW", 1, 0), ("D", 10, 0), ("T", 4, 1),
+    ("T", 5, 0), ("Y", 1, 0), ("QY", 1, 0), ("XW", 2, 0), ("D", 11, 0), ("HE", 3, 0), ("D", 12, 0), ("SQ", 2, 0),
+    ("T", 5, 1), ("E", 4, 0), ("E", 4, 1), ("T", 6, 0), ("RC", 2, 0), ("Y", 2, 0), ("E", 5, 0), ("T", 6, 1),
+    ("QY", 2, 0), ("XW", 3, 0), ("D", 13, 0), ("E", 5, 1), ("T", 7, 0), ("E", 6, 0), ("T", 7, 1), ("D", 14, 0),
+    ("E", 6, 1), ("T", 8, 0), ("E", 7, 0), ("T", 8, 1), ("D", 15, 0), ("E", 7, 1), ("T", 9, 0), ("E", 8, 0),
+    ("T", 9, 1), ("E", 8, 1), ("Q", 4, 0), ("T", 10, 0), ("SQ", 3, 0), ("Q", 5, 0), ("T", 10, 1), ("E", 9, 0),
+    ("RC", 3, 0), ("E", 9, 1), ("Y", 3, 0), ("T", 11, 0), ("E", 10, 0), ("QY", 3, 0), ("T", 11, 1), ("Q", 6, 0),
+    ("M", 0, 0), ("E", 10, 1), ("T", 12, 0), ("Q", 7, 0), ("M", 1, 0), ("E", 11, 0), ("Q", 8, 0), ("T", 12, 1),
+    ("E", 11, 1), ("T", 13, 0), ("Q", 9, 0), ("M", 2, 0), ("E", 12, 0), ("T", 13, 1), ("Q", 10, 0), ("M", 3, 0),
+    ("E", 12, 1), ("T", 14, 0), ("Q", 11, 0), ("E", 13, 0), ("T", 14, 1), ("Q", 12, 0), ("M", 4, 0), ("E", 13, 1),
+    ("T", 15, 0), ("P", 0, 0), ("M", 5, 0), ("P", 1, 0), ("E", 14, 0), ("Q", 13, 0), ("T", 15, 1), ("E", 14, 1),
+    ("M", 6, 0), ("P", 2, 0), ("M", 7, 0), ("P", 3, 0), ("E", 15, 0), ("P", 4, 0), ("M", 8, 0), ("Q", 14, 0),
+    ("M", 9, 0), ("E", 15, 1), ("P", 5, 0), ("M", 10, 0), ("P", 6, 0), ("R", 0, 0), ("M", 11, 0), ("P", 7, 0),
+    ("Q", 15, 0), ("M", 12, 0), ("R", 1, 0), ("M", 13, 0), ("P", 8, 0), ("M", 14, 0), ("P", 9, 0), ("P", 10, 0),
+    ("M", 15, 0), ("P", 11, 0), ("P", 12, 0), ("R", 2, 0), ("P", 13, 0), ("P", 14, 0), ("P", 15, 0), ("R", 3, 0),
+)
+
+
+def tile_gcnclassifer_pb_kernel(tc, h_gcn1, adj, gcn2_w, gcn2_b, out):
+    nc = tc.nc
+    with ExitStack() as ctx:
+        keep = ctx.enter_context(tc.tile_pool(name="keep", bufs=1))
+        stage = ctx.enter_context(tc.tile_pool(name="stage", bufs=8))
+        junk = ctx.enter_context(tc.tile_pool(name="junk", bufs=2))
+        small = ctx.enter_context(tc.tile_pool(name="small", bufs=4))
+        ps_t = ctx.enter_context(tc.psum_pool(name="ps_t", bufs=4))
+        ps_x = ctx.enter_context(tc.psum_pool(name="ps_x", bufs=1))
+        ps_o = ctx.enter_context(tc.psum_pool(name="ps_o", bufs=2))
+        ctx.enter_context(tc.manual_schedule())
+
+        one = keep.tile([P, 1], F32)
+        nc.vector.memset(one[:], 1.0)
+        warm = keep.tile([P, 1], F32)
+        nc.scalar.sqrt(out=warm[:], in_=one[:])
+        ident = keep.tile([P, P], F32)
+        make_identity(nc, ident[:])
+
+        a_tiles = []
+        for b in range(TILES // 2):
+            a_t = keep.tile([P, 2, N_NODES], BF16, name="adj%d" % b)
+            a_tiles.append(a_t)
+        w_sb = keep.tile([P, 2, G_OUT], BF16)
+        h_sb = keep.tile([P, TILES // 2, 2, H_IN], BF16)
+        bias = keep.tile([P, G_OUT], BF16)
+
+        nc.scalar.dma_start(out=bias[:], in_=gcn2_b.partition_broadcast(P))
+        for r in range(TILES):
+            rows = adj[256 * (r // 2) : 256 * (r // 2) + 256, :].rearrange("(p e) j -> p e j", e=2)
+            nc.sync.dma_start(out=a_tiles[r // 2][:, r % 2, :], in_=rows[:, r % 2, :])
+            if r == H_AFTER:
+                nc.sync.dma_start(out=w_sb[:], in_=gcn2_w.rearrange("(q k) g -> q k g", k=2))
+                nc.sync.dma_start(
+                    out=h_sb[:].rearrange("p b e k -> p b (e k)"),
+                    in_=h_gcn1.rearrange("(b p e) k -> p b (e k)", p=P, e=2),
+                )
+
+        deg = keep.tile([P, TILES, 8], F32)
+        dis = keep.tile([P, TILES], F32)
+        codes = keep.tile([P, TILES, 512], U32, align_bytes=64)
+        scales = keep.tile([P, TILES, 512], U8, align_bytes=64)
+        h_t = keep.tile([P, TILES, P], F32)
+        y_g = keep.tile([P, PASSES, G_OUT, 4], BF16, align_bytes=64)
+        y_codes = keep.tile([P, PASSES, G_OUT], U32, align_bytes=64)
+        y_scales = keep.tile([P, PASSES, G_OUT], U8, align_bytes=64)
+        z_sb = keep.tile([P, TILES, G_OUT], F32)
+        o_sb = keep.tile([P, TILES, G_OUT], F32)
+        out_v = out.rearrange("(b p e) g -> p b (e g)", p=P, e=2)
+
+        live = {}
+
+        def degree(r):
+            src = a_tiles[r // 2][:, r % 2, :]
+            acc = deg[:, r, 0:1]
+            if D_MODE[r] == "S":
+                js = junk.tile([P, N_NODES], BF16)
+                nc.scalar.activation(out=js[:], in_=src, func=ACT.Copy, accum_out=acc)
+            else:
+                jv = junk.tile([P, N_NODES], BF16)
+                nc.vector.tensor_scalar(
+                    out=jv[:], in0=src, scalar1=1.0, scalar2=None, op0=ALU.mult, op1=ALU.add, accum_out=acc
+                )
+
+        def flip(r, half):
+            words = a_tiles[r // 2][:].bitcast(F32)[:, r % 2, :]
+            xt = ps_t.tile([P, 2, 2, P], F32, name="xt")
+            live[("xt", r, half)] = xt
+            for cc in range(2):
+                for u in range(2):
+                    first = 256 * (2 * half + cc) + 128 * u
+                    nc.tensor.transpose(xt[:, cc, u, :], words[:, first : first + 128], ident[:])
+
+        def evacuate(r, half):
+            if ("g", r) not in live:
+                g_t = stage.tile([P, 4 * 512], BF16, align_bytes=64, name="g_t")
+                live[("g", r)] = g_t
+            g_w = live[("g", r)][:].bitcast(F32).rearrange("p (c i u) -> p c i u", c=4, u=2)
+            dst = g_w[:, 2 * half : 2 * half + 2, :, :]
+            src = live[("xt", r, half)][:].rearrange("p c u i -> p c i u")
+            if E_ENG[r][half] == "S":
+                nc.scalar.copy(out=dst, in_=src)
+            else:
+                nc.vector.tensor_copy(out=dst, in_=src)
+
+        def quantise(r):
+            nc.vector.quantize_mx(
+                out=codes[:, r, :].bitcast(FP8X4), scales=scales[:, r, :], in_=live[("g", r)][:]
+            )
+
+        def flip_h(q):
+            h_w = h_sb[:].bitcast(F32)
+            ht = ps_t.tile([P, 4, P], F32, name="xt")
+            live[("ht", q)] = ht
+            for t in range(4):
+                r = 4 * q + t
+                nc.tensor.transpose(ht[:, t, :], h_w[:, r // 2, r % 2, :], ident[:])
+
+        def evacuate_h(q):
+            nc.scalar.copy(out=h_t[:, 4 * q : 4 * q + 4, :], in_=live[("ht", q)][:])
+
+        def root(c):
+            rt = small.tile([P, 4], F32, name="rt")
+            live[("rt", c)] = rt
+            n = 0
+            if n > 0:
+                nc.scalar.sqrt(out=rt[:, 0:n], in_=live[("d2", c)][:, 0:n])
+            if n < 4:
+                nc.scalar.sqrt(out=rt[:, n:4], in_=deg[:, 4 * c + n : 4 * c + 4, 0])
+
+        def recip(c):
+            nc.vector.reciprocal(out=dis[:, 4 * c : 4 * c + 4], in_=live[("rt", c)][:])
+
+        def project(c):
+            h_b = h_t[:].bitcast(BF16).rearrange("p r (j k) -> p r j k", k=2)
+            xw = ps_x.tile([P, 4, G_OUT], F32, name="xw")
+            live[("xw", c)] = xw
+            for t in range(4):
+                for k in range(2):
+                    nc.tensor.matmul(
+                        out=xw[:, t, :],
+                        lhsT=h_b[:, 4 * c + t, :, k],
+                        rhs=w_sb[:, k, :],
+                        start=(k == 0),
+                        stop=(k == 1),
+                    )
+
+        def scale_y(c):
+            nc.vector.tensor_tensor(
+                out=y_g[:, c, :, :],
+                in0=live[("xw", c)][:].rearrange("p t g -> p g t"),
+                in1=dis[:, 4 * c : 4 * c + 4].unsqueeze(1).to_broadcast([P, G_OUT, 4]),
+                op=ALU.mult,
+            )
+
+        def quantise_y(c):
+            nc.vector.quantize_mx(
+                out=y_codes[:, c, :].bitcast(FP8X4),
+                scales=y_scales[:, c, :],
+                in_=y_g[:, c, :, :].rearrange("p g t -> p (g t)"),
+            )
+
+        def multiply(r):
+            if ("acc", r // 4) not in live:
+                acc_ps = ps_o.tile([P, 4, G_OUT], F32, name="acc_ps")
+                live[("acc", r // 4)] = acc_ps
+            for c in range(PASSES):
+                nc.tensor.matmul_mx(
+                    out=live[("acc", r // 4)][:, r % 4, :],
+                    lhsT=codes[:, r, 128 * c : 128 * c + 128].bitcast(FP8X4),
+                    lhsT_scale=scales[:, r, 128 * c : 128 * c + 128],
+                    rhs=y_codes[:, c, :].bitcast(FP8X4),
+                    rhs_scale=y_scales[:, c, :],
+                    start=(c == 0),
+                    stop=(c == PASSES - 1),
+                )
+
+        def finish(r):
+            nc.vector.scalar_tensor_tensor(
+                out=z_sb[:, r, :],
+                in0=live[("acc", r // 4)][:, r % 4, :],
+                scalar=dis[:, r : r + 1],
+                in1=bias[:],
+                op0=ALU.mult,
+                op1=ALU.add,
+            )
+
+        def relu_store(m):
+            nc.scalar.activation(
+                out=o_sb[:, 4 * m : 4 * m + 4, :], in_=z_sb[:, 4 * m : 4 * m + 4, :], func=ACT.Relu
+            )
+            nc.sync.dma_start(
+                out=out_v[:, 2 * m : 2 * m + 2, :],
+                in_=o_sb[:, 4 * m : 4 * m + 4, :].rearrange("p (b e) g -> p b (e g)", e=2),
+            )
+
+        for kind, a, b in ORDER:
+            if kind == "D":
+                degree(a)
+            elif kind == "T":
+                flip(a, b)
+            elif kind == "E":
+                evacuate(a, b)
+            elif kind == "Q":
+                quantise(a)
+            elif kind == "HT":
+                flip_h(a)
+            elif kind == "HE":
+                evacuate_h(a)
+            elif kind == "SQ":
+                root(a)
+            elif kind == "RC":
+                recip(a)
+            elif kind == "XW":
+                project(a)
+            elif kind == "Y":
+                scale_y(a)
+            elif kind == "QY":
+                quantise_y(a)
+            elif kind == "M":
+                multiply(a)
+            elif kind == "P":
+                finish(a)
+            elif kind == "R":
+                relu_store(a)
+            else:
+                assert False, kind

@@ -106,9 +106,15 @@ def tile_gcnclassifer_pb_kernel(tc, h_gcn1, adj, gcn2_w, gcn2_b, out):
                 js = junk.tile([P, N_NODES], BF16)
                 nc.scalar.activation(out=js[:], in_=src, func=ACT.Copy, accum_out=acc)
             else:
-                jv = junk.tile([P, N_NODES], BF16)
-                nc.vector.tensor_scalar(
-                    out=jv[:], in0=src, scalar1=1.0, scalar2=None, op0=ALU.mult, op1=ALU.add, accum_out=acc
+                jv = junk.tile([P, N_NODES // 2], F32)
+                nc.vector.scalar_tensor_tensor(
+                    out=jv[:],
+                    in0=src[:, 0 : N_NODES // 2],
+                    scalar=1.0,
+                    in1=src[:, N_NODES // 2 : N_NODES],
+                    op0=ALU.mult,
+                    op1=ALU.add,
+                    accum_out=acc,
                 )
 
         def flip(r, half):

@@ -20,30 +20,32 @@ PASSES = 4
 
 FLOPS = 2 * N_NODES * N_NODES * G_OUT + 2 * N_NODES * H_IN * G_OUT
 
-D_MODE = "VSVVSVVSVVSVVVVV"
+D_MODE = "VVSVVVSVVVSVVVVV"
 E_ENG = ("SS", "SS", "SS", "SS", "SS", "SS", "SS", "SS", "SS", "SS", "SS", "SS", "SS", "SS", "SS", "SS")
-H_AFTER = 3
+H_AFTER = 1
 ORDER = (
-    ("T", 0, 0), ("D", 0, 0), ("T", 0, 1), ("E", 0, 0), ("T", 1, 0), ("D", 1, 0), ("T", 1, 1), ("T", 2, 0),
-    ("D", 2, 0), ("E", 0, 1), ("D", 3, 0), ("E", 1, 0), ("T", 2, 1), ("E", 1, 1), ("Q", 0, 0), ("T", 3, 0),
-    ("SQ", 0, 0), ("T", 3, 1), ("Q", 1, 0), ("E", 2, 0), ("RC", 0, 0), ("E", 2, 1), ("HT", 0, 0), ("E", 3, 0),
-    ("HT", 1, 0), ("Q", 2, 0), ("D", 4, 0), ("HT", 2, 0), ("D", 5, 0), ("E", 3, 1), ("D", 6, 0), ("HE", 0, 0),
-    ("HT", 3, 0), ("D", 7, 0), ("Q", 3, 0), ("XW", 0, 0), ("T", 4, 0), ("Y", 0, 0), ("QY", 0, 0), ("D", 8, 0),
-    ("SQ", 1, 0), ("HE", 1, 0), ("RC", 1, 0), ("HE", 2, 0), ("D", 9, 0), ("XW", 1, 0), ("D", 10, 0), ("T", 4, 1),
-    ("T", 5, 0), ("Y", 1, 0), ("QY", 1, 0), ("XW", 2, 0), ("D", 11, 0), ("HE", 3, 0), ("D", 12, 0), ("SQ", 2, 0),
-    ("T", 5, 1), ("E", 4, 0), ("E", 4, 1), ("T", 6, 0), ("RC", 2, 0), ("Y", 2, 0), ("E", 5, 0), ("T", 6, 1),
-    ("QY", 2, 0), ("XW", 3, 0), ("D", 13, 0), ("E", 5, 1), ("T", 7, 0), ("E", 6, 0), ("T", 7, 1), ("D", 14, 0),
-    ("E", 6, 1), ("T", 8, 0), ("E", 7, 0), ("T", 8, 1), ("D", 15, 0), ("E", 7, 1), ("T", 9, 0), ("E", 8, 0),
-    ("T", 9, 1), ("E", 8, 1), ("Q", 4, 0), ("T", 10, 0), ("SQ", 3, 0), ("Q", 5, 0), ("T", 10, 1), ("E", 9, 0),
-    ("RC", 3, 0), ("E", 9, 1), ("Y", 3, 0), ("T", 11, 0), ("E", 10, 0), ("QY", 3, 0), ("T", 11, 1), ("Q", 6, 0),
-    ("M", 0, 0), ("E", 10, 1), ("T", 12, 0), ("Q", 7, 0), ("M", 1, 0), ("E", 11, 0), ("Q", 8, 0), ("T", 12, 1),
-    ("E", 11, 1), ("T", 13, 0), ("Q", 9, 0), ("M", 2, 0), ("E", 12, 0), ("T", 13, 1), ("Q", 10, 0), ("M", 3, 0),
-    ("E", 12, 1), ("T", 14, 0), ("Q", 11, 0), ("E", 13, 0), ("T", 14, 1), ("Q", 12, 0), ("M", 4, 0), ("E", 13, 1),
-    ("T", 15, 0), ("P", 0, 0), ("M", 5, 0), ("P", 1, 0), ("E", 14, 0), ("Q", 13, 0), ("T", 15, 1), ("E", 14, 1),
-    ("M", 6, 0), ("P", 2, 0), ("M", 7, 0), ("P", 3, 0), ("E", 15, 0), ("P", 4, 0), ("M", 8, 0), ("Q", 14, 0),
-    ("M", 9, 0), ("E", 15, 1), ("P", 5, 0), ("M", 10, 0), ("P", 6, 0), ("R", 0, 0), ("M", 11, 0), ("P", 7, 0),
-    ("Q", 15, 0), ("M", 12, 0), ("R", 1, 0), ("M", 13, 0), ("P", 8, 0), ("M", 14, 0), ("P", 9, 0), ("P", 10, 0),
-    ("M", 15, 0), ("P", 11, 0), ("P", 12, 0), ("R", 2, 0), ("P", 13, 0), ("P", 14, 0), ("P", 15, 0), ("R", 3, 0),
+    ("T", 0, 0), ("D", 0, 0), ("T", 0, 1), ("E", 0, 0), ("D", 1, 0), ("T", 1, 0), ("E", 0, 1), ("T", 1, 1),
+    ("E", 1, 0), ("Q", 0, 0), ("E", 1, 1), ("HT", 0, 0), ("Q", 1, 0), ("HT", 1, 0), ("HE", 0, 0), ("T", 2, 0),
+    ("D", 2, 0), ("HE", 1, 0), ("XW", 0, 0), ("D", 3, 0), ("XW", 1, 0), ("XW", 2, 0), ("XW", 3, 0), ("XW", 4, 0),
+    ("D", 4, 0), ("XW", 5, 0), ("SQ", 0, 0), ("T", 2, 1), ("E", 2, 0), ("XW", 6, 0), ("T", 3, 0), ("E", 2, 1),
+    ("RC", 0, 0), ("HT", 2, 0), ("Y", 0, 0), ("T", 3, 1), ("E", 3, 0), ("HT", 3, 0), ("QY", 0, 0), ("D", 5, 0),
+    ("XW", 7, 0), ("D", 6, 0), ("T", 5, 0), ("HE", 3, 0), ("D", 7, 0), ("T", 4, 1), ("HE", 2, 0), ("D", 8, 0),
+    ("SQ", 1, 0), ("T", 4, 0), ("E", 3, 1), ("XW", 8, 0), ("E", 4, 1), ("T", 5, 1), ("RC", 1, 0), ("Y", 1, 0),
+    ("E", 4, 0), ("XW", 9, 0), ("QY", 1, 0), ("D", 10, 0), ("D", 9, 0), ("T", 6, 0), ("T", 6, 1), ("D", 11, 0),
+    ("XW", 10, 0), ("XW", 11, 0), ("XW", 12, 0), ("XW", 13, 0), ("E", 5, 0), ("XW", 14, 0), ("D", 12, 0), ("XW", 15, 0),
+    ("SQ", 2, 0), ("T", 7, 0), ("E", 5, 1), ("E", 6, 0), ("T", 7, 1), ("RC", 2, 0), ("Y", 2, 0), ("E", 6, 1),
+    ("T", 8, 0), ("QY", 2, 0), ("D", 13, 0), ("E", 7, 0), ("T", 8, 1), ("E", 7, 1), ("T", 9, 0), ("D", 14, 0),
+    ("E", 8, 0), ("T", 9, 1), ("E", 8, 1), ("T", 10, 0), ("D", 15, 0), ("E", 9, 0), ("T", 10, 1), ("E", 9, 1),
+    ("T", 11, 0), ("Q", 2, 0), ("SQ", 3, 0), ("T", 11, 1), ("RC", 3, 0), ("E", 10, 0), ("Y", 3, 0), ("E", 10, 1),
+    ("T", 12, 0), ("QY", 3, 0), ("Q", 3, 0), ("T", 12, 1), ("Q", 4, 0), ("E", 11, 0), ("Q", 5, 0), ("E", 11, 1),
+    ("T", 13, 0), ("Q", 6, 0), ("E", 12, 0), ("T", 13, 1), ("Q", 7, 0), ("E", 12, 1), ("T", 14, 0), ("E", 13, 0),
+    ("Q", 8, 0), ("T", 14, 1), ("E", 13, 1), ("Q", 9, 0), ("T", 15, 0), ("E", 14, 0), ("Q", 10, 0), ("T", 15, 1),
+    ("E", 14, 1), ("Q", 11, 0), ("E", 15, 0), ("M", 0, 0), ("Q", 12, 0), ("E", 15, 1), ("Q", 13, 0), ("M", 1, 0),
+    ("P", 0, 0), ("Q", 14, 0), ("M", 2, 0), ("P", 1, 0), ("M", 3, 0), ("Q", 15, 0), ("M", 4, 0), ("P", 2, 0),
+    ("P", 3, 0), ("M", 5, 0), ("R", 0, 0), ("P", 4, 0), ("M", 6, 0), ("P", 5, 0), ("M", 7, 0), ("P", 6, 0),
+    ("M", 8, 0), ("P", 7, 0), ("M", 9, 0), ("R", 1, 0), ("P", 8, 0), ("M", 10, 0), ("P", 9, 0), ("M", 11, 0),
+    ("P", 10, 0), ("M", 12, 0), ("P", 11, 0), ("M", 13, 0), ("R", 2, 0), ("P", 12, 0), ("M", 14, 0), ("P", 13, 0),
+    ("M", 15, 0), ("P", 14, 0), ("P", 15, 0), ("R", 3, 0),
 )
 
 
@@ -55,7 +57,7 @@ def tile_gcnclassifer_pb_kernel(tc, h_gcn1, adj, gcn2_w, gcn2_b, out):
         junk = ctx.enter_context(tc.tile_pool(name="junk", bufs=2))
         small = ctx.enter_context(tc.tile_pool(name="small", bufs=4))
         ps_t = ctx.enter_context(tc.psum_pool(name="ps_t", bufs=4))
-        ps_x = ctx.enter_context(tc.psum_pool(name="ps_x", bufs=1))
+        ps_x = ctx.enter_context(tc.psum_pool(name="ps_x", bufs=2))
         ps_o = ctx.enter_context(tc.psum_pool(name="ps_o", bufs=2))
         ctx.enter_context(tc.manual_schedule())
 
@@ -106,15 +108,9 @@ def tile_gcnclassifer_pb_kernel(tc, h_gcn1, adj, gcn2_w, gcn2_b, out):
                 js = junk.tile([P, N_NODES], BF16)
                 nc.scalar.activation(out=js[:], in_=src, func=ACT.Copy, accum_out=acc)
             else:
-                jv = junk.tile([P, N_NODES // 2], F32)
-                nc.vector.scalar_tensor_tensor(
-                    out=jv[:],
-                    in0=src[:, 0 : N_NODES // 2],
-                    scalar=1.0,
-                    in1=src[:, N_NODES // 2 : N_NODES],
-                    op0=ALU.mult,
-                    op1=ALU.add,
-                    accum_out=acc,
+                jv = junk.tile([P, N_NODES], BF16)
+                nc.vector.tensor_scalar(
+                    out=jv[:], in0=src, scalar1=1.0, scalar2=None, op0=ALU.mult, op1=ALU.add, accum_out=acc
                 )
 
         def flip(r, half):
@@ -152,7 +148,10 @@ def tile_gcnclassifer_pb_kernel(tc, h_gcn1, adj, gcn2_w, gcn2_b, out):
                 nc.tensor.transpose(ht[:, t, :], h_w[:, r // 2, r % 2, :], ident[:])
 
         def evacuate_h(q):
-            nc.scalar.copy(out=h_t[:, 4 * q : 4 * q + 4, :], in_=live[("ht", q)][:])
+            if q % 2 == 0:
+                nc.scalar.copy(out=h_t[:, 4 * q : 4 * q + 4, :], in_=live[("ht", q)][:])
+            else:
+                nc.vector.tensor_copy(out=h_t[:, 4 * q : 4 * q + 4, :], in_=live[("ht", q)][:])
 
         def root(c):
             rt = small.tile([P, 4], F32, name="rt")
@@ -166,19 +165,19 @@ def tile_gcnclassifer_pb_kernel(tc, h_gcn1, adj, gcn2_w, gcn2_b, out):
         def recip(c):
             nc.vector.reciprocal(out=dis[:, 4 * c : 4 * c + 4], in_=live[("rt", c)][:])
 
-        def project(c):
+        def project(r):
             h_b = h_t[:].bitcast(BF16).rearrange("p r (j k) -> p r j k", k=2)
-            xw = ps_x.tile([P, 4, G_OUT], F32, name="xw")
-            live[("xw", c)] = xw
-            for t in range(4):
-                for k in range(2):
-                    nc.tensor.matmul(
-                        out=xw[:, t, :],
-                        lhsT=h_b[:, 4 * c + t, :, k],
-                        rhs=w_sb[:, k, :],
-                        start=(k == 0),
-                        stop=(k == 1),
-                    )
+            if ("xw", r // 4) not in live:
+                xw = ps_x.tile([P, 4, G_OUT], F32, name="xw")
+                live[("xw", r // 4)] = xw
+            for k in range(2):
+                nc.tensor.matmul(
+                    out=live[("xw", r // 4)][:, r % 4, :],
+                    lhsT=h_b[:, r, :, k],
+                    rhs=w_sb[:, k, :],
+                    start=(k == 0),
+                    stop=(k == 1),
+                )
 
         def scale_y(c):
             nc.vector.tensor_tensor(

@@ -17,36 +17,12 @@ H_IN = 256
 G_OUT = 128
 TILES = 16
 PASSES = 4
+HALF = N_NODES // 2
 
 FLOPS = 2 * N_NODES * N_NODES * G_OUT + 2 * N_NODES * H_IN * G_OUT
 
-D_MODE = "VVSVVVSVVVSVVVVV"
-E_ENG = ("SS", "SS", "SS", "SS", "SS", "SS", "SS", "SS", "SS", "SS", "SS", "SS", "SS", "SS", "SS", "SS")
-H_AFTER = 1
-ORDER = (
-    ("T", 0, 0), ("D", 0, 0), ("T", 0, 1), ("E", 0, 0), ("D", 1, 0), ("T", 1, 0), ("E", 0, 1), ("T", 1, 1),
-    ("E", 1, 0), ("Q", 0, 0), ("E", 1, 1), ("HT", 0, 0), ("Q", 1, 0), ("HT", 1, 0), ("HE", 0, 0), ("T", 2, 0),
-    ("D", 2, 0), ("HE", 1, 0), ("XW", 0, 0), ("D", 3, 0), ("XW", 1, 0), ("XW", 2, 0), ("XW", 3, 0), ("XW", 4, 0),
-    ("D", 4, 0), ("XW", 5, 0), ("SQ", 0, 0), ("T", 2, 1), ("E", 2, 0), ("XW", 6, 0), ("T", 3, 0), ("E", 2, 1),
-    ("RC", 0, 0), ("HT", 2, 0), ("Y", 0, 0), ("T", 3, 1), ("E", 3, 0), ("HT", 3, 0), ("QY", 0, 0), ("D", 5, 0),
-    ("XW", 7, 0), ("D", 6, 0), ("T", 5, 0), ("HE", 3, 0), ("D", 7, 0), ("T", 4, 1), ("HE", 2, 0), ("D", 8, 0),
-    ("SQ", 1, 0), ("T", 4, 0), ("E", 3, 1), ("XW", 8, 0), ("E", 4, 1), ("T", 5, 1), ("RC", 1, 0), ("Y", 1, 0),
-    ("E", 4, 0), ("XW", 9, 0), ("QY", 1, 0), ("D", 10, 0), ("D", 9, 0), ("T", 6, 0), ("T", 6, 1), ("D", 11, 0),
-    ("XW", 10, 0), ("XW", 11, 0), ("XW", 12, 0), ("XW", 13, 0), ("E", 5, 0), ("XW", 14, 0), ("D", 12, 0), ("XW", 15, 0),
-    ("SQ", 2, 0), ("T", 7, 0), ("E", 5, 1), ("E", 6, 0), ("T", 7, 1), ("RC", 2, 0), ("Y", 2, 0), ("E", 6, 1),
-    ("T", 8, 0), ("QY", 2, 0), ("D", 13, 0), ("E", 7, 0), ("T", 8, 1), ("E", 7, 1), ("T", 9, 0), ("D", 14, 0),
-    ("E", 8, 0), ("T", 9, 1), ("E", 8, 1), ("T", 10, 0), ("D", 15, 0), ("E", 9, 0), ("T", 10, 1), ("E", 9, 1),
-    ("T", 11, 0), ("Q", 2, 0), ("SQ", 3, 0), ("T", 11, 1), ("RC", 3, 0), ("E", 10, 0), ("Y", 3, 0), ("E", 10, 1),
-    ("T", 12, 0), ("QY", 3, 0), ("Q", 3, 0), ("T", 12, 1), ("Q", 4, 0), ("E", 11, 0), ("Q", 5, 0), ("E", 11, 1),
-    ("T", 13, 0), ("Q", 6, 0), ("E", 12, 0), ("T", 13, 1), ("Q", 7, 0), ("E", 12, 1), ("T", 14, 0), ("E", 13, 0),
-    ("Q", 8, 0), ("T", 14, 1), ("E", 13, 1), ("Q", 9, 0), ("T", 15, 0), ("E", 14, 0), ("Q", 10, 0), ("T", 15, 1),
-    ("E", 14, 1), ("Q", 11, 0), ("E", 15, 0), ("M", 0, 0), ("Q", 12, 0), ("E", 15, 1), ("Q", 13, 0), ("M", 1, 0),
-    ("P", 0, 0), ("Q", 14, 0), ("M", 2, 0), ("P", 1, 0), ("M", 3, 0), ("Q", 15, 0), ("M", 4, 0), ("P", 2, 0),
-    ("P", 3, 0), ("M", 5, 0), ("R", 0, 0), ("P", 4, 0), ("M", 6, 0), ("P", 5, 0), ("M", 7, 0), ("P", 6, 0),
-    ("M", 8, 0), ("P", 7, 0), ("M", 9, 0), ("R", 1, 0), ("P", 8, 0), ("M", 10, 0), ("P", 9, 0), ("M", 11, 0),
-    ("P", 10, 0), ("M", 12, 0), ("P", 11, 0), ("M", 13, 0), ("R", 2, 0), ("P", 12, 0), ("M", 14, 0), ("P", 13, 0),
-    ("M", 15, 0), ("P", 14, 0), ("P", 15, 0), ("R", 3, 0),
-)
+SCALAR_DEGREES = (2, 6, 10)
+H_AFTER = 3
 
 
 def tile_gcnclassifer_pb_kernel(tc, h_gcn1, adj, gcn2_w, gcn2_b, out):
@@ -56,10 +32,9 @@ def tile_gcnclassifer_pb_kernel(tc, h_gcn1, adj, gcn2_w, gcn2_b, out):
         stage = ctx.enter_context(tc.tile_pool(name="stage", bufs=8))
         junk = ctx.enter_context(tc.tile_pool(name="junk", bufs=2))
         small = ctx.enter_context(tc.tile_pool(name="small", bufs=4))
-        ps_t = ctx.enter_context(tc.psum_pool(name="ps_t", bufs=4))
-        ps_x = ctx.enter_context(tc.psum_pool(name="ps_x", bufs=2))
-        ps_o = ctx.enter_context(tc.psum_pool(name="ps_o", bufs=2))
-        ctx.enter_context(tc.manual_schedule())
+        ps_t = ctx.enter_context(tc.psum_pool(name="ps_t", bufs=3))
+        ps_x = ctx.enter_context(tc.psum_pool(name="ps_x", bufs=1))
+        ps_o = ctx.enter_context(tc.psum_pool(name="ps_o", bufs=1))
 
         one = keep.tile([P, 1], F32)
         nc.vector.memset(one[:], 1.0)
@@ -68,24 +43,22 @@ def tile_gcnclassifer_pb_kernel(tc, h_gcn1, adj, gcn2_w, gcn2_b, out):
         ident = keep.tile([P, P], F32)
         make_identity(nc, ident[:])
 
-        a_tiles = []
-        for b in range(TILES // 2):
-            a_t = keep.tile([P, 2, N_NODES], BF16, name="adj%d" % b)
-            a_tiles.append(a_t)
+        a_sb = keep.tile([P, TILES, N_NODES], BF16)
         w_sb = keep.tile([P, 2, G_OUT], BF16)
-        h_sb = keep.tile([P, TILES // 2, 2, H_IN], BF16)
+        h_sb = keep.tile([P, TILES, H_IN], BF16)
         bias = keep.tile([P, G_OUT], BF16)
 
-        nc.scalar.dma_start(out=bias[:], in_=gcn2_b.partition_broadcast(P))
+        adj_v = adj.rearrange("(b p e) j -> p b e j", p=P, e=2)
         for r in range(TILES):
-            rows = adj[256 * (r // 2) : 256 * (r // 2) + 256, :].rearrange("(p e) j -> p e j", e=2)
-            nc.sync.dma_start(out=a_tiles[r // 2][:, r % 2, :], in_=rows[:, r % 2, :])
+            nc.sync.dma_start(out=a_sb[:, r, :], in_=adj_v[:, r // 2, r % 2, :])
             if r == H_AFTER:
                 nc.sync.dma_start(out=w_sb[:], in_=gcn2_w.rearrange("(q k) g -> q k g", k=2))
                 nc.sync.dma_start(
-                    out=h_sb[:].rearrange("p b e k -> p b (e k)"),
+                    out=h_sb[:].rearrange("p (b e) k -> p b (e k)", e=2),
                     in_=h_gcn1.rearrange("(b p e) k -> p b (e k)", p=P, e=2),
                 )
+
+        nc.sync.dma_start(out=bias[:], in_=gcn2_b.partition_broadcast(P))
 
         deg = keep.tile([P, TILES, 8], F32)
         dis = keep.tile([P, TILES], F32)
@@ -98,128 +71,111 @@ def tile_gcnclassifer_pb_kernel(tc, h_gcn1, adj, gcn2_w, gcn2_b, out):
         z_sb = keep.tile([P, TILES, G_OUT], F32)
         o_sb = keep.tile([P, TILES, G_OUT], F32)
         out_v = out.rearrange("(b p e) g -> p b (e g)", p=P, e=2)
-
-        live = {}
+        grouped = {}
 
         def degree(r):
-            src = a_tiles[r // 2][:, r % 2, :]
             acc = deg[:, r, 0:1]
-            if D_MODE[r] == "S":
+            if r in SCALAR_DEGREES:
                 js = junk.tile([P, N_NODES], BF16)
-                nc.scalar.activation(out=js[:], in_=src, func=ACT.Copy, accum_out=acc)
+                nc.scalar.activation(out=js[:], in_=a_sb[:, r, :], func=ACT.Copy, accum_out=acc)
             else:
-                jv = junk.tile([P, N_NODES], BF16)
-                nc.vector.tensor_scalar(
-                    out=jv[:], in0=src, scalar1=1.0, scalar2=None, op0=ALU.mult, op1=ALU.add, accum_out=acc
+                jv = junk.tile([P, HALF], F32)
+                nc.vector.scalar_tensor_tensor(
+                    out=jv[:],
+                    in0=a_sb[:, r, 0:HALF],
+                    scalar=1.0,
+                    in1=a_sb[:, r, HALF:N_NODES],
+                    op0=ALU.mult,
+                    op1=ALU.add,
+                    accum_out=acc,
                 )
 
-        def flip(r, half):
-            words = a_tiles[r // 2][:].bitcast(F32)[:, r % 2, :]
-            xt = ps_t.tile([P, 2, 2, P], F32, name="xt")
-            live[("xt", r, half)] = xt
-            for cc in range(2):
-                for u in range(2):
-                    first = 256 * (2 * half + cc) + 128 * u
-                    nc.tensor.transpose(xt[:, cc, u, :], words[:, first : first + 128], ident[:])
-
-        def evacuate(r, half):
-            if ("g", r) not in live:
-                g_t = stage.tile([P, 4 * 512], BF16, align_bytes=64, name="g_t")
-                live[("g", r)] = g_t
-            g_w = live[("g", r)][:].bitcast(F32).rearrange("p (c i u) -> p c i u", c=4, u=2)
-            dst = g_w[:, 2 * half : 2 * half + 2, :, :]
-            src = live[("xt", r, half)][:].rearrange("p c u i -> p c i u")
-            if E_ENG[r][half] == "S":
-                nc.scalar.copy(out=dst, in_=src)
-            else:
-                nc.vector.tensor_copy(out=dst, in_=src)
+        def flip(r):
+            words = a_sb[:, r, :].bitcast(F32)
+            g_t = stage.tile([P, 4 * 512], BF16, align_bytes=64, name="g_t")
+            grouped[r] = g_t
+            g_w = g_t[:].bitcast(F32).rearrange("p (c i u) -> p c i u", c=4, u=2)
+            for half in range(2):
+                xt = ps_t.tile([P, 2, 2, P], F32, name="xt")
+                for cc in range(2):
+                    for u in range(2):
+                        first = 256 * (2 * half + cc) + 128 * u
+                        nc.tensor.transpose(xt[:, cc, u, :], words[:, first : first + 128], ident[:])
+                nc.scalar.copy(
+                    out=g_w[:, 2 * half : 2 * half + 2, :, :], in_=xt[:].rearrange("p c u i -> p c i u")
+                )
 
         def quantise(r):
             nc.vector.quantize_mx(
-                out=codes[:, r, :].bitcast(FP8X4), scales=scales[:, r, :], in_=live[("g", r)][:]
+                out=codes[:, r, :].bitcast(FP8X4), scales=scales[:, r, :], in_=grouped[r][:]
             )
 
-        def flip_h(q):
+        def flip_h():
             h_w = h_sb[:].bitcast(F32)
-            ht = ps_t.tile([P, 4, P], F32, name="xt")
-            live[("ht", q)] = ht
-            for t in range(4):
-                r = 4 * q + t
-                nc.tensor.transpose(ht[:, t, :], h_w[:, r // 2, r % 2, :], ident[:])
+            for q in range(PASSES):
+                ht = ps_t.tile([P, 4, P], F32, name="xt")
+                for t in range(4):
+                    nc.tensor.transpose(ht[:, t, :], h_w[:, 4 * q + t, :], ident[:])
+                nc.scalar.copy(out=h_t[:, 4 * q : 4 * q + 4, :], in_=ht[:])
 
-        def evacuate_h(q):
-            if q % 2 == 0:
-                nc.scalar.copy(out=h_t[:, 4 * q : 4 * q + 4, :], in_=live[("ht", q)][:])
-            else:
-                nc.vector.tensor_copy(out=h_t[:, 4 * q : 4 * q + 4, :], in_=live[("ht", q)][:])
-
-        def root(c):
+        def make_y(c):
             rt = small.tile([P, 4], F32, name="rt")
-            live[("rt", c)] = rt
-            n = 0
-            if n > 0:
-                nc.scalar.sqrt(out=rt[:, 0:n], in_=live[("d2", c)][:, 0:n])
-            if n < 4:
-                nc.scalar.sqrt(out=rt[:, n:4], in_=deg[:, 4 * c + n : 4 * c + 4, 0])
-
-        def recip(c):
-            nc.vector.reciprocal(out=dis[:, 4 * c : 4 * c + 4], in_=live[("rt", c)][:])
-
-        def project(r):
+            nc.scalar.sqrt(out=rt[:], in_=deg[:, 4 * c : 4 * c + 4, 0])
+            nc.vector.reciprocal(out=dis[:, 4 * c : 4 * c + 4], in_=rt[:])
             h_b = h_t[:].bitcast(BF16).rearrange("p r (j k) -> p r j k", k=2)
-            if ("xw", r // 4) not in live:
-                xw = ps_x.tile([P, 4, G_OUT], F32, name="xw")
-                live[("xw", r // 4)] = xw
-            for k in range(2):
-                nc.tensor.matmul(
-                    out=live[("xw", r // 4)][:, r % 4, :],
-                    lhsT=h_b[:, r, :, k],
-                    rhs=w_sb[:, k, :],
-                    start=(k == 0),
-                    stop=(k == 1),
-                )
-
-        def scale_y(c):
+            xw = ps_x.tile([P, 4, G_OUT], F32, name="xw")
+            for t in range(4):
+                for k in range(2):
+                    nc.tensor.matmul(
+                        out=xw[:, t, :],
+                        lhsT=h_b[:, 4 * c + t, :, k],
+                        rhs=w_sb[:, k, :],
+                        start=(k == 0),
+                        stop=(k == 1),
+                    )
             nc.vector.tensor_tensor(
                 out=y_g[:, c, :, :],
-                in0=live[("xw", c)][:].rearrange("p t g -> p g t"),
+                in0=xw[:].rearrange("p t g -> p g t"),
                 in1=dis[:, 4 * c : 4 * c + 4].unsqueeze(1).to_broadcast([P, G_OUT, 4]),
                 op=ALU.mult,
             )
-
-        def quantise_y(c):
             nc.vector.quantize_mx(
                 out=y_codes[:, c, :].bitcast(FP8X4),
                 scales=y_scales[:, c, :],
                 in_=y_g[:, c, :, :].rearrange("p g t -> p (g t)"),
             )
 
-        def multiply(r):
-            if ("acc", r // 4) not in live:
-                acc_ps = ps_o.tile([P, 4, G_OUT], F32, name="acc_ps")
-                live[("acc", r // 4)] = acc_ps
-            for c in range(PASSES):
+        acc = []
+        for m in range(PASSES):
+            acc_ps = ps_o.tile([P, 4, G_OUT], F32, name="acc%d" % m)
+            acc.append(acc_ps)
+
+        issued = set()
+
+        def passes(m, c):
+            for t in range(4):
+                r = 4 * m + t
                 nc.tensor.matmul_mx(
-                    out=live[("acc", r // 4)][:, r % 4, :],
+                    out=acc[m][:, t, :],
                     lhsT=codes[:, r, 128 * c : 128 * c + 128].bitcast(FP8X4),
                     lhsT_scale=scales[:, r, 128 * c : 128 * c + 128],
                     rhs=y_codes[:, c, :].bitcast(FP8X4),
                     rhs_scale=y_scales[:, c, :],
-                    start=(c == 0),
-                    stop=(c == PASSES - 1),
+                    start=(c == 0 and t == 0),
+                    stop=(c == PASSES - 1 and t == 3),
                 )
 
-        def finish(r):
-            nc.vector.scalar_tensor_tensor(
-                out=z_sb[:, r, :],
-                in0=live[("acc", r // 4)][:, r % 4, :],
-                scalar=dis[:, r : r + 1],
-                in1=bias[:],
-                op0=ALU.mult,
-                op1=ALU.add,
-            )
-
-        def relu_store(m):
+        def epilogue(m):
+            for t in range(4):
+                r = 4 * m + t
+                nc.vector.scalar_tensor_tensor(
+                    out=z_sb[:, r, :],
+                    in0=acc[m][:, t, :],
+                    scalar=dis[:, r : r + 1],
+                    in1=bias[:],
+                    op0=ALU.mult,
+                    op1=ALU.add,
+                )
             nc.scalar.activation(
                 out=o_sb[:, 4 * m : 4 * m + 4, :], in_=z_sb[:, 4 * m : 4 * m + 4, :], func=ACT.Relu
             )
@@ -228,34 +184,22 @@ def tile_gcnclassifer_pb_kernel(tc, h_gcn1, adj, gcn2_w, gcn2_b, out):
                 in_=o_sb[:, 4 * m : 4 * m + 4, :].rearrange("p (b e) g -> p b (e g)", e=2),
             )
 
-        for kind, a, b in ORDER:
-            if kind == "D":
-                degree(a)
-            elif kind == "T":
-                flip(a, b)
-            elif kind == "E":
-                evacuate(a, b)
-            elif kind == "Q":
-                quantise(a)
-            elif kind == "HT":
-                flip_h(a)
-            elif kind == "HE":
-                evacuate_h(a)
-            elif kind == "SQ":
-                root(a)
-            elif kind == "RC":
-                recip(a)
-            elif kind == "XW":
-                project(a)
-            elif kind == "Y":
-                scale_y(a)
-            elif kind == "QY":
-                quantise_y(a)
-            elif kind == "M":
-                multiply(a)
-            elif kind == "P":
-                finish(a)
-            elif kind == "R":
-                relu_store(a)
-            else:
-                assert False, kind
+        for c in range(PASSES + 1):
+            if c < PASSES:
+                for r in range(4 * c, 4 * c + 4):
+                    degree(r)
+                    flip(r)
+                    if r == H_AFTER:
+                        flip_h()
+                make_y(c)
+            if c > 0:
+                for r in range(4 * c - 4, 4 * c):
+                    quantise(r)
+                known = min(c, PASSES - 1) + 1
+                for m in range(c):
+                    for k in range(known):
+                        if (m, k) not in issued:
+                            passes(m, k)
+                            issued.add((m, k))
+        for m in range(PASSES):
+            epilogue(m)

@@ -32,9 +32,8 @@ def tile_gcnclassifer_pb_kernel(tc, h_gcn1, adj, gcn2_w, gcn2_b, out):
         stage = ctx.enter_context(tc.tile_pool(name="stage", bufs=8))
         junk = ctx.enter_context(tc.tile_pool(name="junk", bufs=2))
         small = ctx.enter_context(tc.tile_pool(name="small", bufs=4))
-        ps_t = ctx.enter_context(tc.psum_pool(name="ps_t", bufs=3))
+        ps_t = ctx.enter_context(tc.psum_pool(name="ps_t", bufs=7))
         ps_x = ctx.enter_context(tc.psum_pool(name="ps_x", bufs=1))
-        ps_o = ctx.enter_context(tc.psum_pool(name="ps_o", bufs=1))
 
         one = keep.tile([P, 1], F32)
         nc.vector.memset(one[:], 1.0)
@@ -50,7 +49,11 @@ def tile_gcnclassifer_pb_kernel(tc, h_gcn1, adj, gcn2_w, gcn2_b, out):
 
         adj_v = adj.rearrange("(b p e) j -> p b e j", p=P, e=2)
         for r in range(TILES):
-            nc.sync.dma_start(out=a_sb[:, r, :], in_=adj_v[:, r // 2, r % 2, :])
+            if r == 0:
+                nc.sync.dma_start(out=a_sb[:, r, 0:HALF], in_=adj_v[:, 0, 0, 0:HALF])
+                nc.sync.dma_start(out=a_sb[:, r, HALF:N_NODES], in_=adj_v[:, 0, 0, HALF:N_NODES])
+            else:
+                nc.sync.dma_start(out=a_sb[:, r, :], in_=adj_v[:, r // 2, r % 2, :])
             if r == H_AFTER:
                 nc.sync.dma_start(out=w_sb[:], in_=gcn2_w.rearrange("(q k) g -> q k g", k=2))
                 nc.sync.dma_start(
@@ -145,14 +148,14 @@ def tile_gcnclassifer_pb_kernel(tc, h_gcn1, adj, gcn2_w, gcn2_b, out):
                 in_=y_g[:, c, :, :].rearrange("p g t -> p (g t)"),
             )
 
-        acc = []
-        for m in range(PASSES):
-            acc_ps = ps_o.tile([P, 4, G_OUT], F32, name="acc%d" % m)
-            acc.append(acc_ps)
+        acc = {}
 
         issued = set()
 
         def passes(m, c):
+            if m not in acc:
+                acc_ps = ps_t.tile([P, 4, G_OUT], F32, name="xt")
+                acc[m] = acc_ps
             for t in range(4):
                 r = 4 * m + t
                 nc.tensor.matmul_mx(

@@ -47,6 +47,7 @@ def tile_gcnclassifer_pb_kernel(tc, h_gcn1, adj, gcn2_w, gcn2_b, out):
         h_sb = keep.tile([P, TILES, H_IN], BF16)
         bias = keep.tile([P, G_OUT], BF16)
 
+        nc.scalar.dma_start(out=bias[:], in_=gcn2_b.partition_broadcast(P))
         adj_v = adj.rearrange("(b p e) j -> p b e j", p=P, e=2)
         for r in range(TILES):
             if r == 0:
@@ -60,8 +61,6 @@ def tile_gcnclassifer_pb_kernel(tc, h_gcn1, adj, gcn2_w, gcn2_b, out):
                     out=h_sb[:].rearrange("p (b e) k -> p b (e k)", e=2),
                     in_=h_gcn1.rearrange("(b p e) k -> p b (e k)", p=P, e=2),
                 )
-
-        nc.sync.dma_start(out=bias[:], in_=gcn2_b.partition_broadcast(P))
 
         deg = keep.tile([P, TILES, 8], F32)
         dis = keep.tile([P, TILES], F32)

from contextlib import ExitStack

import concourse.mybir as mybir
from concourse.masks import make_identity

F32 = mybir.dt.float32
BF16 = mybir.dt.bfloat16
U32 = mybir.dt.uint32
U8 = mybir.dt.uint8
FP8X4 = mybir.dt.float8_e4m3fn_x4
ALU = mybir.AluOpType
ACT = mybir.ActivationFunctionType

P = 128
N_NODES = 2048
H_IN = 256
G_OUT = 128
TILES = 16
PASSES = 4
HALF = N_NODES // 2

FLOPS = 2 * N_NODES * N_NODES * G_OUT + 2 * N_NODES * H_IN * G_OUT

SCALAR_DEGREES = (2, 6, 10)
H_AFTER = 3


def tile_gcnclassifer_pb_kernel(tc, h_gcn1, adj, gcn2_w, gcn2_b, out):
    nc = tc.nc
    with ExitStack() as ctx:
        keep = ctx.enter_context(tc.tile_pool(name="keep", bufs=1))
        stage = ctx.enter_context(tc.tile_pool(name="stage", bufs=8))
        junk = ctx.enter_context(tc.tile_pool(name="junk", bufs=2))
        small = ctx.enter_context(tc.tile_pool(name="small", bufs=4))
        ps_t = ctx.enter_context(tc.psum_pool(name="ps_t", bufs=7))
        ps_x = ctx.enter_context(tc.psum_pool(name="ps_x", bufs=1))

        one = keep.tile([P, 1], F32)
        nc.vector.memset(one[:], 1.0)
        warm = keep.tile([P, 1], F32)
        nc.scalar.sqrt(out=warm[:], in_=one[:])
        ident = keep.tile([P, P], F32)
        make_identity(nc, ident[:])

        a_sb = keep.tile([P, TILES, N_NODES], BF16)
        w_sb = keep.tile([P, 2, G_OUT], BF16)
        h_sb = keep.tile([P, TILES, H_IN], BF16)
        bias = keep.tile([P, G_OUT], BF16)

        nc.scalar.dma_start(out=bias[:], in_=gcn2_b.partition_broadcast(P))
        adj_v = adj.rearrange("(b p e) j -> p b e j", p=P, e=2)
        for r in range(TILES):
            if r == 0:
                nc.sync.dma_start(out=a_sb[:, r, 0:HALF], in_=adj_v[:, 0, 0, 0:HALF])
                nc.sync.dma_start(out=a_sb[:, r, HALF:N_NODES], in_=adj_v[:, 0, 0, HALF:N_NODES])
            else:
                nc.sync.dma_start(out=a_sb[:, r, :], in_=adj_v[:, r // 2, r % 2, :])
            if r == H_AFTER:
                nc.sync.dma_start(out=w_sb[:], in_=gcn2_w.rearrange("(q k) g -> q k g", k=2))
                nc.sync.dma_start(
                    out=h_sb[:].rearrange("p (b e) k -> p b (e k)", e=2),
                    in_=h_gcn1.rearrange("(b p e) k -> p b (e k)", p=P, e=2),
                )

        deg = keep.tile([P, TILES, 8], F32)
        dis = keep.tile([P, TILES], F32)
        codes = keep.tile([P, TILES, 512], U32, align_bytes=64)
        scales = keep.tile([P, TILES, 512], U8, align_bytes=64)
        h_t = keep.tile([P, TILES, P], F32)
        y_g = keep.tile([P, PASSES, G_OUT, 4], BF16, align_bytes=64)
        y_codes = keep.tile([P, PASSES, G_OUT], U32, align_bytes=64)
        y_scales = keep.tile([P, PASSES, G_OUT], U8, align_bytes=64)
        z_sb = keep.tile([P, TILES, G_OUT], F32)
        o_sb = keep.tile([P, TILES, G_OUT], F32)
        out_v = out.rearrange("(b p e) g -> p b (e g)", p=P, e=2)
        grouped = {}

        def degree(r):
            acc = deg[:, r, 0:1]
            if r in SCALAR_DEGREES:
                js = junk.tile([P, N_NODES], BF16)
                nc.scalar.activation(out=js[:], in_=a_sb[:, r, :], func=ACT.Copy, accum_out=acc)
            else:
                jv = junk.tile([P, HALF], F32)
                nc.vector.scalar_tensor_tensor(
                    out=jv[:],
                    in0=a_sb[:, r, 0:HALF],
                    scalar=1.0,
                    in1=a_sb[:, r, HALF:N_NODES],
                    op0=ALU.mult,
                    op1=ALU.add,
                    accum_out=acc,
                )

        def flip(r):
            words = a_sb[:, r, :].bitcast(F32)
            g_t = stage.tile([P, 4 * 512], BF16, align_bytes=64, name="g_t")
            grouped[r] = g_t
            g_w = g_t[:].bitcast(F32).rearrange("p (c i u) -> p c i u", c=4, u=2)
            for half in range(2):
                xt = ps_t.tile([P, 2, 2, P], F32, name="xt")
                for cc in range(2):
                    for u in range(2):
                        first = 256 * (2 * half + cc) + 128 * u
                        nc.tensor.transpose(xt[:, cc, u, :], words[:, first : first + 128], ident[:])
                nc.scalar.copy(
                    out=g_w[:, 2 * half : 2 * half + 2, :, :], in_=xt[:].rearrange("p c u i -> p c i u")
                )

        def quantise(r):
            nc.vector.quantize_mx(
                out=codes[:, r, :].bitcast(FP8X4), scales=scales[:, r, :], in_=grouped[r][:]
            )

        def flip_h():
            h_w = h_sb[:].bitcast(F32)
            for q in range(PASSES):
                ht = ps_t.tile([P, 4, P], F32, name="xt")
                for t in range(4):
                    nc.tensor.transpose(ht[:, t, :], h_w[:, 4 * q + t, :], ident[:])
                nc.scalar.copy(out=h_t[:, 4 * q : 4 * q + 4, :], in_=ht[:])

        def make_y(c):
            rt = small.tile([P, 4], F32, name="rt")
            nc.scalar.sqrt(out=rt[:], in_=deg[:, 4 * c : 4 * c + 4, 0])
            nc.vector.reciprocal(out=dis[:, 4 * c : 4 * c + 4], in_=rt[:])
            h_b = h_t[:].bitcast(BF16).rearrange("p r (j k) -> p r j k", k=2)
            xw = ps_x.tile([P, 4, G_OUT], F32, name="xw")
            for t in range(4):
                for k in range(2):
                    nc.tensor.matmul(
                        out=xw[:, t, :],
                        lhsT=h_b[:, 4 * c + t, :, k],
                        rhs=w_sb[:, k, :],
                        start=(k == 0),
                        stop=(k == 1),
                    )
            nc.vector.tensor_tensor(
                out=y_g[:, c, :, :],
                in0=xw[:].rearrange("p t g -> p g t"),
                in1=dis[:, 4 * c : 4 * c + 4].unsqueeze(1).to_broadcast([P, G_OUT, 4]),
                op=ALU.mult,
            )
            nc.vector.quantize_mx(
                out=y_codes[:, c, :].bitcast(FP8X4),
                scales=y_scales[:, c, :],
                in_=y_g[:, c, :, :].rearrange("p g t -> p (g t)"),
            )

        acc = {}

        issued = set()

        def passes(m, c):
            if m not in acc:
                acc_ps = ps_t.tile([P, 4, G_OUT], F32, name="xt")
                acc[m] = acc_ps
            for t in range(4):
                r = 4 * m + t
                nc.tensor.matmul_mx(
                    out=acc[m][:, t, :],
                    lhsT=codes[:, r, 128 * c : 128 * c + 128].bitcast(FP8X4),
                    lhsT_scale=scales[:, r, 128 * c : 128 * c + 128],
                    rhs=y_codes[:, c, :].bitcast(FP8X4),
                    rhs_scale=y_scales[:, c, :],
                    start=(c == 0 and t == 0),
                    stop=(c == PASSES - 1 and t == 3),
                )

        def epilogue(m):
            for t in range(4):
                r = 4 * m + t
                nc.vector.scalar_tensor_tensor(
                    out=z_sb[:, r, :],
                    in0=acc[m][:, t, :],
                    scalar=dis[:, r : r + 1],
                    in1=bias[:],
                    op0=ALU.mult,
                    op1=ALU.add,
                )
            nc.scalar.activation(
                out=o_sb[:, 4 * m : 4 * m + 4, :], in_=z_sb[:, 4 * m : 4 * m + 4, :], func=ACT.Relu
            )
            nc.sync.dma_start(
                out=out_v[:, 2 * m : 2 * m + 2, :],
                in_=o_sb[:, 4 * m : 4 * m + 4, :].rearrange("p (b e) g -> p b (e g)", e=2),
            )

        for c in range(PASSES + 1):
            if c < PASSES:
                for r in range(4 * c, 4 * c + 4):
                    degree(r)
                    flip(r)
                    if r == H_AFTER:
                        flip_h()
                make_y(c)
            if c > 0:
                for r in range(4 * c - 4, 4 * c):
                    quantise(r)
                known = min(c, PASSES - 1) + 1
                for m in range(c):
                    for k in range(known):
                        if (m, k) not in issued:
                            passes(m, k)
                            issued.add((m, k))
        for m in range(PASSES):
            epilogue(m)
